import numpy as np
import ml_dtypes

BF16 = ml_dtypes.bfloat16


def bf(x):
    return np.asarray(x, np.float32).astype(BF16)


def f32(x):
    return np.asarray(x, np.float32)


def f64(x):
    return np.asarray(x).astype(np.float64)


def striped(idx):
    return np.tile(idx.reshape(-1, 16).T, (8, 1))


C, S, T, N, H, K = 128, 256, 8, 2048, 128, 16


def sigmoid(v):
    return 1.0 / (1.0 + np.exp(-v))


def setup_inputs():
    x = f32(np.sqrt(2.0 / np.sqrt(C)) * np.random.standard_normal((C, S)))
    idx = np.concatenate([np.random.permutation(S)[:H] for _ in range(K)])
    return {"x": x, "offs": striped(idx)}


def reference(x, offs):
    idx = offs[:16].T.reshape(-1)
    xv = f64(x)
    prod = xv[:, idx] * np.tile(xv, (1, T))
    return sigmoid(prod.sum(axis=0, keepdims=True))

@@ -1,0 +1,54 @@
+import concourse.mybir as mybir
+
+F32 = mybir.dt.float32
+U16 = mybir.dt.uint16
+
+FEATURES = 128
+NODES = 256
+PARTNERS = 8
+LIST = NODES * PARTNERS
+OFFSETS_PER_COLUMN = 16
+PIECE_COLUMNS = NODES // OFFSETS_PER_COLUMN
+
+FLOPS = 2 * FEATURES * LIST
+
+
+def tile_crossentropy_kernel(tc, x, offs, out):
+    nc = tc.nc
+    with (
+        tc.tile_pool(name="held", bufs=1) as held,
+        tc.psum_pool(name="psum", bufs=1) as psum,
+    ):
+        offsets = held.tile([FEATURES, LIST // OFFSETS_PER_COLUMN], U16, name="offsets")
+        nc.sync.dma_start(offsets[:], offs)
+
+        window = held.tile([FEATURES, NODES], F32, name="window")
+        nc.scalar.dma_start(window[:], x)
+        own = held.tile([FEATURES, NODES], F32, name="own")
+        nc.sync.dma_start(own[:], x)
+
+        selector = held.tile([FEATURES, 2 * PARTNERS - 1], F32, name="selector")
+        nc.gpsimd.memset(selector[:], 0.0)
+        nc.gpsimd.memset(selector[:, PARTNERS - 1 : PARTNERS], 1.0)
+
+        products = held.tile([FEATURES, LIST], F32, name="products")
+        sums = psum.tile([PARTNERS, NODES], F32, name="sums")
+        for t in range(PARTNERS):
+            piece = products[:, t * NODES : (t + 1) * NODES]
+            nc.vector.tensor_tensor(
+                piece,
+                window[:].indirect(offsets[:, t * PIECE_COLUMNS : (t + 1) * PIECE_COLUMNS]),
+                own[:],
+                mybir.AluOpType.mult,
+            )
+            nc.tensor.matmul(
+                sums[:],
+                selector[:, PARTNERS - 1 - t : 2 * PARTNERS - 1 - t],
+                piece,
+                start=(t == 0),
+                stop=(t == PARTNERS - 1),
+            )
+
+        scores = held.tile([PARTNERS, NODES], F32, name="scores")
+        nc.scalar.activation(scores[:], sums[:], mybir.ActivationFunctionType.Sigmoid)
+        nc.scalar.dma_start(out.rearrange("o (t n) -> (o t) n", t=PARTNERS), scores[:])

@@ -10,6 +10,9 @@ LIST = NODES * PARTNERS
 OFFSETS_PER_COLUMN = 16
 PIECE_COLUMNS = NODES // OFFSETS_PER_COLUMN
 
+WARMING_COLUMNS = 128
+WARMING_MATMULS = 6
+
 FLOPS = 2 * FEATURES * LIST
 
 
@@ -30,6 +33,12 @@ def tile_crossentropy_kernel(tc, x, offs, out):
         selector = held.tile([FEATURES, 2 * PARTNERS - 1], F32, name="selector")
         nc.gpsimd.memset(selector[:], 0.0)
         nc.gpsimd.memset(selector[:, PARTNERS - 1 : PARTNERS], 1.0)
+
+        zeros = held.tile([FEATURES, WARMING_COLUMNS], F32, name="zeros")
+        nc.vector.memset(zeros[:], 0.0)
+        discarded = psum.tile([PARTNERS, WARMING_COLUMNS], F32, name="discarded")
+        for i in range(WARMING_MATMULS):
+            nc.tensor.matmul(discarded[:], selector[:, 0:PARTNERS], zeros[:], start=True, stop=True)
 
         products = held.tile([FEATURES, LIST], F32, name="products")
         sums = psum.tile([PARTNERS, NODES], F32, name="sums")

@@ -5,13 +5,11 @@ U16 = mybir.dt.uint16
 
 FEATURES = 128
 NODES = 256
-PARTNERS = 8
-LIST = NODES * PARTNERS
+LIST = 2048
+PIECE = 128
+PIECES = LIST // PIECE
 OFFSETS_PER_COLUMN = 16
-PIECE_COLUMNS = NODES // OFFSETS_PER_COLUMN
-
-WARMING_COLUMNS = 128
-WARMING_MATMULS = 6
+PIECE_COLUMNS = PIECE // OFFSETS_PER_COLUMN
 
 FLOPS = 2 * FEATURES * LIST
 
@@ -30,34 +28,29 @@ def tile_crossentropy_kernel(tc, x, offs, out):
         own = held.tile([FEATURES, NODES], F32, name="own")
         nc.sync.dma_start(own[:], x)
 
-        selector = held.tile([FEATURES, 2 * PARTNERS - 1], F32, name="selector")
+        selector = held.tile([FEATURES, 2 * PIECES - 1], F32, name="selector")
         nc.gpsimd.memset(selector[:], 0.0)
-        nc.gpsimd.memset(selector[:, PARTNERS - 1 : PARTNERS], 1.0)
-
-        zeros = held.tile([FEATURES, WARMING_COLUMNS], F32, name="zeros")
-        nc.vector.memset(zeros[:], 0.0)
-        discarded = psum.tile([PARTNERS, WARMING_COLUMNS], F32, name="discarded")
-        for i in range(WARMING_MATMULS):
-            nc.tensor.matmul(discarded[:], selector[:, 0:PARTNERS], zeros[:], start=True, stop=True)
+        nc.gpsimd.memset(selector[:, PIECES - 1 : PIECES], 1.0)
 
         products = held.tile([FEATURES, LIST], F32, name="products")
-        sums = psum.tile([PARTNERS, NODES], F32, name="sums")
-        for t in range(PARTNERS):
-            piece = products[:, t * NODES : (t + 1) * NODES]
+        sums = psum.tile([PIECES, PIECE], F32, name="sums")
+        for k in range(PIECES):
+            first_node = (k * PIECE) % NODES
+            piece = products[:, k * PIECE : (k + 1) * PIECE]
             nc.vector.tensor_tensor(
                 piece,
-                window[:].indirect(offsets[:, t * PIECE_COLUMNS : (t + 1) * PIECE_COLUMNS]),
-                own[:],
+                window[:].indirect(offsets[:, k * PIECE_COLUMNS : (k + 1) * PIECE_COLUMNS]),
+                own[:, first_node : first_node + PIECE],
                 mybir.AluOpType.mult,
             )
             nc.tensor.matmul(
                 sums[:],
-                selector[:, PARTNERS - 1 - t : 2 * PARTNERS - 1 - t],
+                selector[:, PIECES - 1 - k : 2 * PIECES - 1 - k],
                 piece,
-                start=(t == 0),
-                stop=(t == PARTNERS - 1),
+                start=(k == 0),
+                stop=(k == PIECES - 1),
             )
 
-        scores = held.tile([PARTNERS, NODES], F32, name="scores")
+        scores = held.tile([PIECES, PIECE], F32, name="scores")
         nc.scalar.activation(scores[:], sums[:], mybir.ActivationFunctionType.Sigmoid)
-        nc.scalar.dma_start(out.rearrange("o (t n) -> (o t) n", t=PARTNERS), scores[:])
+        nc.scalar.dma_start(out.rearrange("o (k n) -> (o k) n", k=PIECES), scores[:])

@@ -11,6 +11,8 @@ PIECES = LIST // PIECE
 OFFSETS_PER_COLUMN = 16
 PIECE_COLUMNS = PIECE // OFFSETS_PER_COLUMN
 
+WARMING_MATMULS = 6
+
 FLOPS = 2 * FEATURES * LIST
 
 
@@ -31,6 +33,12 @@ def tile_crossentropy_kernel(tc, x, offs, out):
         selector = held.tile([FEATURES, 2 * PIECES - 1], F32, name="selector")
         nc.gpsimd.memset(selector[:], 0.0)
         nc.gpsimd.memset(selector[:, PIECES - 1 : PIECES], 1.0)
+
+        zeros = held.tile([FEATURES, PIECE], F32, name="zeros")
+        nc.vector.memset(zeros[:], 0.0)
+        discarded = psum.tile([PIECES, PIECE], F32, name="discarded")
+        for i in range(WARMING_MATMULS):
+            nc.tensor.matmul(discarded[:], selector[:, 0:PIECES], zeros[:], start=True, stop=True)
 
         products = held.tile([FEATURES, LIST], F32, name="products")
         sums = psum.tile([PIECES, PIECE], F32, name="sums")

@@ -5,12 +5,12 @@ U16 = mybir.dt.uint16
 
 FEATURES = 128
 NODES = 256
-LIST = 2048
-PIECE = 128
-PIECES = LIST // PIECE
+PARTNERS = 8
+LIST = NODES * PARTNERS
 OFFSETS_PER_COLUMN = 16
-PIECE_COLUMNS = PIECE // OFFSETS_PER_COLUMN
+PIECE_SIZES = [NODES] * (PARTNERS - 1) + [NODES // 2] * 2
 
+WARMING_COLUMNS = 128
 WARMING_MATMULS = 6
 
 FLOPS = 2 * FEATURES * LIST
@@ -30,35 +30,38 @@ def tile_crossentropy_kernel(tc, x, offs, out):
         own = held.tile([FEATURES, NODES], F32, name="own")
         nc.sync.dma_start(own[:], x)
 
-        selector = held.tile([FEATURES, 2 * PIECES - 1], F32, name="selector")
+        selector = held.tile([FEATURES, 2 * PARTNERS - 1], F32, name="selector")
         nc.gpsimd.memset(selector[:], 0.0)
-        nc.gpsimd.memset(selector[:, PIECES - 1 : PIECES], 1.0)
+        nc.gpsimd.memset(selector[:, PARTNERS - 1 : PARTNERS], 1.0)
 
-        zeros = held.tile([FEATURES, PIECE], F32, name="zeros")
+        zeros = held.tile([FEATURES, WARMING_COLUMNS], F32, name="zeros")
         nc.vector.memset(zeros[:], 0.0)
-        discarded = psum.tile([PIECES, PIECE], F32, name="discarded")
+        discarded = psum.tile([PARTNERS, WARMING_COLUMNS], F32, name="discarded")
         for i in range(WARMING_MATMULS):
-            nc.tensor.matmul(discarded[:], selector[:, 0:PIECES], zeros[:], start=True, stop=True)
+            nc.tensor.matmul(discarded[:], selector[:, 0:PARTNERS], zeros[:], start=True, stop=True)
 
         products = held.tile([FEATURES, LIST], F32, name="products")
-        sums = psum.tile([PIECES, PIECE], F32, name="sums")
-        for k in range(PIECES):
-            first_node = (k * PIECE) % NODES
-            piece = products[:, k * PIECE : (k + 1) * PIECE]
+        sums = psum.tile([PARTNERS, NODES], F32, name="sums")
+        begin = 0
+        for size in PIECE_SIZES:
+            end = begin + size
+            t, node = divmod(begin, NODES)
+            piece = products[:, begin:end]
             nc.vector.tensor_tensor(
                 piece,
-                window[:].indirect(offsets[:, k * PIECE_COLUMNS : (k + 1) * PIECE_COLUMNS]),
-                own[:, first_node : first_node + PIECE],
+                window[:].indirect(offsets[:, begin // OFFSETS_PER_COLUMN : end // OFFSETS_PER_COLUMN]),
+                own[:, node : node + size],
                 mybir.AluOpType.mult,
             )
             nc.tensor.matmul(
-                sums[:],
-                selector[:, PIECES - 1 - k : 2 * PIECES - 1 - k],
+                sums[:, node : node + size],
+                selector[:, PARTNERS - 1 - t : 2 * PARTNERS - 1 - t],
                 piece,
-                start=(k == 0),
-                stop=(k == PIECES - 1),
+                start=(begin == 0),
+                stop=(end == LIST),
             )
+            begin = end
 
-        scores = held.tile([PIECES, PIECE], F32, name="scores")
+        scores = held.tile([PARTNERS, NODES], F32, name="scores")
         nc.scalar.activation(scores[:], sums[:], mybir.ActivationFunctionType.Sigmoid)
-        nc.scalar.dma_start(out.rearrange("o (k n) -> (o k) n", k=PIECES), scores[:])
+        nc.scalar.dma_start(out.rearrange("o (t n) -> (o t) n", t=PARTNERS), scores[:])

@@ -9,6 +9,9 @@ PARTNERS = 8
 LIST = NODES * PARTNERS
 OFFSETS_PER_COLUMN = 16
 PIECE_SIZES = [NODES] * (PARTNERS - 1) + [NODES // 2] * 2
+BANK_COLUMNS = 512
+COLUMN_GROUPS = 4
+GROUP_PARTITIONS = 32
 
 WARMING_COLUMNS = 128
 WARMING_MATMULS = 6
@@ -20,7 +23,8 @@ def tile_crossentropy_kernel(tc, x, offs, out):
     nc = tc.nc
     with (
         tc.tile_pool(name="held", bufs=1) as held,
-        tc.psum_pool(name="psum", bufs=1) as psum,
+        tc.psum_pool(name="warming", bufs=1) as warming,
+        tc.psum_pool(name="banks", bufs=COLUMN_GROUPS) as banks,
     ):
         offsets = held.tile([FEATURES, LIST // OFFSETS_PER_COLUMN], U16, name="offsets")
         nc.sync.dma_start(offsets[:], offs)
@@ -30,38 +34,37 @@ def tile_crossentropy_kernel(tc, x, offs, out):
         own = held.tile([FEATURES, NODES], F32, name="own")
         nc.sync.dma_start(own[:], x)
 
-        selector = held.tile([FEATURES, 2 * PARTNERS - 1], F32, name="selector")
-        nc.gpsimd.memset(selector[:], 0.0)
-        nc.gpsimd.memset(selector[:, PARTNERS - 1 : PARTNERS], 1.0)
+        ones = held.tile([FEATURES, 1], F32, name="ones")
+        nc.gpsimd.memset(ones[:], 1.0)
 
         zeros = held.tile([FEATURES, WARMING_COLUMNS], F32, name="zeros")
         nc.vector.memset(zeros[:], 0.0)
-        discarded = psum.tile([PARTNERS, WARMING_COLUMNS], F32, name="discarded")
+        discarded = warming.tile([1, BANK_COLUMNS], F32, name="discarded")
         for i in range(WARMING_MATMULS):
-            nc.tensor.matmul(discarded[:], selector[:, 0:PARTNERS], zeros[:], start=True, stop=True)
+            nc.tensor.matmul(discarded[:, 0:WARMING_COLUMNS], ones[:], zeros[:], start=True, stop=True)
 
         products = held.tile([FEATURES, LIST], F32, name="products")
-        sums = psum.tile([PARTNERS, NODES], F32, name="sums")
+        scores = held.tile([FEATURES, LIST], F32, name="scores")
         begin = 0
-        for size in PIECE_SIZES:
+        for k, size in enumerate(PIECE_SIZES):
             end = begin + size
-            t, node = divmod(begin, NODES)
-            piece = products[:, begin:end]
+            node = begin % NODES
+            row = (k % COLUMN_GROUPS) * GROUP_PARTITIONS
             nc.vector.tensor_tensor(
-                piece,
+                products[:, begin:end],
                 window[:].indirect(offsets[:, begin // OFFSETS_PER_COLUMN : end // OFFSETS_PER_COLUMN]),
                 own[:, node : node + size],
                 mybir.AluOpType.mult,
             )
+            sums = banks.tile([FEATURES, BANK_COLUMNS], F32, name="sums")
             nc.tensor.matmul(
-                sums[:, node : node + size],
-                selector[:, PARTNERS - 1 - t : 2 * PARTNERS - 1 - t],
-                piece,
-                start=(begin == 0),
-                stop=(end == LIST),
+                sums[row : row + 1, 0:size], ones[:], products[:, begin:end], start=True, stop=True
             )
+            nc.scalar.activation(
+                scores[row : row + 1, begin:end],
+                sums[row : row + 1, 0:size],
+                mybir.ActivationFunctionType.Sigmoid,
+            )
+            queue = nc.scalar if end == LIST else nc.sync
+            queue.dma_start(out[:, begin:end], scores[row : row + 1, begin:end])
             begin = end
-
-        scores = held.tile([PARTNERS, NODES], F32, name="scores")
-        nc.scalar.activation(scores[:], sums[:], mybir.ActivationFunctionType.Sigmoid)
-        nc.scalar.dma_start(out.rearrange("o (t n) -> (o t) n", t=PARTNERS), scores[:])

@@ -8,10 +8,12 @@ NODES = 256
 PARTNERS = 8
 LIST = NODES * PARTNERS
 OFFSETS_PER_COLUMN = 16
-PIECE_SIZES = [NODES] * (PARTNERS - 1) + [NODES // 2] * 2
+WHOLE = [NODES]
+LAST_CUT = [NODES // 2, NODES // 2]
 BANK_COLUMNS = 512
 COLUMN_GROUPS = 4
 GROUP_PARTITIONS = 32
+PARTNERS_IN_A_GROUP = PARTNERS // COLUMN_GROUPS
 
 WARMING_COLUMNS = 128
 WARMING_MATMULS = 6
@@ -44,27 +46,32 @@ def tile_crossentropy_kernel(tc, x, offs, out):
             nc.tensor.matmul(discarded[:, 0:WARMING_COLUMNS], ones[:], zeros[:], start=True, stop=True)
 
         products = held.tile([FEATURES, LIST], F32, name="products")
-        scores = held.tile([FEATURES, LIST], F32, name="scores")
-        begin = 0
-        for k, size in enumerate(PIECE_SIZES):
-            end = begin + size
-            node = begin % NODES
-            row = (k % COLUMN_GROUPS) * GROUP_PARTITIONS
-            nc.vector.tensor_tensor(
-                products[:, begin:end],
-                window[:].indirect(offsets[:, begin // OFFSETS_PER_COLUMN : end // OFFSETS_PER_COLUMN]),
-                own[:, node : node + size],
-                mybir.AluOpType.mult,
-            )
-            sums = banks.tile([FEATURES, BANK_COLUMNS], F32, name="sums")
-            nc.tensor.matmul(
-                sums[row : row + 1, 0:size], ones[:], products[:, begin:end], start=True, stop=True
-            )
-            nc.scalar.activation(
-                scores[row : row + 1, begin:end],
-                sums[row : row + 1, 0:size],
-                mybir.ActivationFunctionType.Sigmoid,
-            )
-            queue = nc.scalar if end == LIST else nc.sync
-            queue.dma_start(out[:, begin:end], scores[row : row + 1, begin:end])
-            begin = end
+        scores = held.tile([FEATURES, PARTNERS_IN_A_GROUP * NODES], F32, name="scores")
+        for t in range(PARTNERS):
+            row = (t % COLUMN_GROUPS) * GROUP_PARTITIONS
+            node = 0
+            for size in LAST_CUT if t == PARTNERS - 1 else WHOLE:
+                begin = t * NODES + node
+                end = begin + size
+                nc.vector.tensor_tensor(
+                    products[:, begin:end],
+                    window[:].indirect(offsets[:, begin // OFFSETS_PER_COLUMN : end // OFFSETS_PER_COLUMN]),
+                    own[:, node : node + size],
+                    mybir.AluOpType.mult,
+                )
+                sums = banks.tile([FEATURES, BANK_COLUMNS], F32, name="sums")
+                nc.tensor.matmul(
+                    sums[row : row + 1, 0:size], ones[:], products[:, begin:end], start=True, stop=True
+                )
+                kept = (t // COLUMN_GROUPS) * NODES + node
+                nc.scalar.activation(
+                    scores[row : row + 1, kept : kept + size],
+                    sums[row : row + 1, 0:size],
+                    mybir.ActivationFunctionType.Sigmoid,
+                )
+                node += size
+
+        nc.scalar.dma_start(
+            out.rearrange("o (a g n) -> (o g) a n", a=PARTNERS_IN_A_GROUP, g=COLUMN_GROUPS),
+            scores[0:FEATURES:GROUP_PARTITIONS, :].rearrange("g (a n) -> g a n", a=PARTNERS_IN_A_GROUP),
+        )

@@ -1,6 +1,7 @@
 import concourse.mybir as mybir
 
 F32 = mybir.dt.float32
+BF16 = mybir.dt.bfloat16
 U16 = mybir.dt.uint16
 
 FEATURES = 128
@@ -15,9 +16,6 @@ COLUMN_GROUPS = 4
 GROUP_PARTITIONS = 32
 PARTNERS_IN_A_GROUP = PARTNERS // COLUMN_GROUPS
 
-WARMING_COLUMNS = 128
-WARMING_MATMULS = 6
-
 FLOPS = 2 * FEATURES * LIST
 
 
@@ -25,7 +23,6 @@ def tile_crossentropy_kernel(tc, x, offs, out):
     nc = tc.nc
     with (
         tc.tile_pool(name="held", bufs=1) as held,
-        tc.psum_pool(name="warming", bufs=1) as warming,
         tc.psum_pool(name="banks", bufs=COLUMN_GROUPS) as banks,
     ):
         offsets = held.tile([FEATURES, LIST // OFFSETS_PER_COLUMN], U16, name="offsets")
@@ -36,16 +33,11 @@ def tile_crossentropy_kernel(tc, x, offs, out):
         own = held.tile([FEATURES, NODES], F32, name="own")
         nc.sync.dma_start(own[:], x)
 
-        ones = held.tile([FEATURES, 1], F32, name="ones")
+        ones = held.tile([FEATURES, 1], BF16, name="ones")
         nc.gpsimd.memset(ones[:], 1.0)
 
-        zeros = held.tile([FEATURES, WARMING_COLUMNS], F32, name="zeros")
-        nc.vector.memset(zeros[:], 0.0)
-        discarded = warming.tile([1, BANK_COLUMNS], F32, name="discarded")
-        for i in range(WARMING_MATMULS):
-            nc.tensor.matmul(discarded[:, 0:WARMING_COLUMNS], ones[:], zeros[:], start=True, stop=True)
-
         products = held.tile([FEATURES, LIST], F32, name="products")
+        halves = products[:].bitcast(BF16)
         scores = held.tile([FEATURES, PARTNERS_IN_A_GROUP * NODES], F32, name="scores")
         for t in range(PARTNERS):
             row = (t % COLUMN_GROUPS) * GROUP_PARTITIONS
@@ -61,7 +53,7 @@ def tile_crossentropy_kernel(tc, x, offs, out):
                 )
                 sums = banks.tile([FEATURES, BANK_COLUMNS], F32, name="sums")
                 nc.tensor.matmul(
-                    sums[row : row + 1, 0:size], ones[:], products[:, begin:end], start=True, stop=True
+                    sums[row : row + 1, 0:size], ones[:], halves[:, 2 * begin + 1 : 2 * end : 2], start=True, stop=True
                 )
                 kept = (t // COLUMN_GROUPS) * NODES + node
                 nc.scalar.activation(

@@ -10,7 +10,7 @@ PARTNERS = 8
 LIST = NODES * PARTNERS
 OFFSETS_PER_COLUMN = 16
 WHOLE = [NODES]
-LAST_CUT = [NODES // 2, NODES // 2]
+LAST_CUT = [NODES // 2, NODES // 4, NODES // 4]
 BANK_COLUMNS = 512
 COLUMN_GROUPS = 4
 GROUP_PARTITIONS = 32

@@ -10,7 +10,8 @@ PARTNERS = 8
 LIST = NODES * PARTNERS
 OFFSETS_PER_COLUMN = 16
 WHOLE = [NODES]
-LAST_CUT = [NODES // 2, NODES // 4, NODES // 4]
+FIRST_CUT = [NODES // 4, NODES - NODES // 4]
+LAST_CUT = [NODES // 2, NODES // 2]
 BANK_COLUMNS = 512
 COLUMN_GROUPS = 4
 GROUP_PARTITIONS = 32
@@ -31,7 +32,8 @@ def tile_crossentropy_kernel(tc, x, offs, out):
         window = held.tile([FEATURES, NODES], F32, name="window")
         nc.scalar.dma_start(window[:], x)
         own = held.tile([FEATURES, NODES], F32, name="own")
-        nc.sync.dma_start(own[:], x)
+        nc.sync.dma_start(own[:, 0 : FIRST_CUT[0]], x[:, 0 : FIRST_CUT[0]])
+        nc.scalar.dma_start(own[:, FIRST_CUT[0] : NODES], x[:, FIRST_CUT[0] : NODES])
 
         ones = held.tile([FEATURES, 1], BF16, name="ones")
         nc.gpsimd.memset(ones[:], 1.0)
@@ -42,7 +44,7 @@ def tile_crossentropy_kernel(tc, x, offs, out):
         for t in range(PARTNERS):
             row = (t % COLUMN_GROUPS) * GROUP_PARTITIONS
             node = 0
-            for size in LAST_CUT if t == PARTNERS - 1 else WHOLE:
+            for size in {0: FIRST_CUT, PARTNERS - 1: LAST_CUT}.get(t, WHOLE):
                 begin = t * NODES + node
                 end = begin + size
                 nc.vector.tensor_tensor(

@@ -13,9 +13,7 @@ WHOLE = [NODES]
 FIRST_CUT = [NODES // 4, NODES - NODES // 4]
 LAST_CUT = [NODES // 2, NODES // 2]
 BANK_COLUMNS = 512
-COLUMN_GROUPS = 4
-GROUP_PARTITIONS = 32
-PARTNERS_IN_A_GROUP = PARTNERS // COLUMN_GROUPS
+BANKS_IN_TURN = 4
 
 FLOPS = 2 * FEATURES * LIST
 
@@ -24,7 +22,7 @@ def tile_crossentropy_kernel(tc, x, offs, out):
     nc = tc.nc
     with (
         tc.tile_pool(name="held", bufs=1) as held,
-        tc.psum_pool(name="banks", bufs=COLUMN_GROUPS) as banks,
+        tc.psum_pool(name="banks", bufs=BANKS_IN_TURN) as banks,
     ):
         offsets = held.tile([FEATURES, LIST // OFFSETS_PER_COLUMN], U16, name="offsets")
         nc.sync.dma_start(offsets[:], offs)
@@ -40,9 +38,8 @@ def tile_crossentropy_kernel(tc, x, offs, out):
 
         products = held.tile([FEATURES, LIST], F32, name="products")
         halves = products[:].bitcast(BF16)
-        scores = held.tile([FEATURES, PARTNERS_IN_A_GROUP * NODES], F32, name="scores")
+        scores = held.tile([1, LIST], F32, name="scores")
         for t in range(PARTNERS):
-            row = (t % COLUMN_GROUPS) * GROUP_PARTITIONS
             node = 0
             for size in {0: FIRST_CUT, PARTNERS - 1: LAST_CUT}.get(t, WHOLE):
                 begin = t * NODES + node
@@ -53,19 +50,13 @@ def tile_crossentropy_kernel(tc, x, offs, out):
                     own[:, node : node + size],
                     mybir.AluOpType.mult,
                 )
-                sums = banks.tile([FEATURES, BANK_COLUMNS], F32, name="sums")
+                sums = banks.tile([1, BANK_COLUMNS], F32, name="sums")
                 nc.tensor.matmul(
-                    sums[row : row + 1, 0:size], ones[:], halves[:, 2 * begin + 1 : 2 * end : 2], start=True, stop=True
+                    sums[:, 0:size], ones[:], halves[:, 2 * begin + 1 : 2 * end : 2], start=True, stop=True
                 )
-                kept = (t // COLUMN_GROUPS) * NODES + node
                 nc.scalar.activation(
-                    scores[row : row + 1, kept : kept + size],
-                    sums[row : row + 1, 0:size],
-                    mybir.ActivationFunctionType.Sigmoid,
+                    scores[:, begin:end], sums[:, 0:size], mybir.ActivationFunctionType.Sigmoid
                 )
                 node += size
 
-        nc.scalar.dma_start(
-            out.rearrange("o (a g n) -> (o g) a n", a=PARTNERS_IN_A_GROUP, g=COLUMN_GROUPS),
-            scores[0:FEATURES:GROUP_PARTITIONS, :].rearrange("g (a n) -> g a n", a=PARTNERS_IN_A_GROUP),
-        )
+        nc.scalar.dma_start(out, scores[:])

@@ -9,9 +9,9 @@ NODES = 256
 PARTNERS = 8
 LIST = NODES * PARTNERS
 OFFSETS_PER_COLUMN = 16
-WHOLE = [NODES]
-FIRST_CUT = [NODES // 4, NODES - NODES // 4]
-LAST_CUT = [NODES // 2, NODES // 2]
+FIRST = NODES // 4
+LAST_CUT = [NODES // 2, NODES // 4]
+PIECES = [FIRST] + (PARTNERS - 1) * [NODES] + LAST_CUT
 BANK_COLUMNS = 512
 BANKS_IN_TURN = 4
 
@@ -30,8 +30,8 @@ def tile_crossentropy_kernel(tc, x, offs, out):
         window = held.tile([FEATURES, NODES], F32, name="window")
         nc.scalar.dma_start(window[:], x)
         own = held.tile([FEATURES, NODES], F32, name="own")
-        nc.sync.dma_start(own[:, 0 : FIRST_CUT[0]], x[:, 0 : FIRST_CUT[0]])
-        nc.scalar.dma_start(own[:, FIRST_CUT[0] : NODES], x[:, FIRST_CUT[0] : NODES])
+        nc.sync.dma_start(own[:, NODES - FIRST : NODES], x[:, 0:FIRST])
+        nc.scalar.dma_start(own[:, 0 : NODES - FIRST], x[:, FIRST:NODES])
 
         ones = held.tile([FEATURES, 1], BF16, name="ones")
         nc.gpsimd.memset(ones[:], 1.0)
@@ -39,24 +39,23 @@ def tile_crossentropy_kernel(tc, x, offs, out):
         products = held.tile([FEATURES, LIST], F32, name="products")
         halves = products[:].bitcast(BF16)
         scores = held.tile([1, LIST], F32, name="scores")
-        for t in range(PARTNERS):
-            node = 0
-            for size in {0: FIRST_CUT, PARTNERS - 1: LAST_CUT}.get(t, WHOLE):
-                begin = t * NODES + node
-                end = begin + size
-                nc.vector.tensor_tensor(
-                    products[:, begin:end],
-                    window[:].indirect(offsets[:, begin // OFFSETS_PER_COLUMN : end // OFFSETS_PER_COLUMN]),
-                    own[:, node : node + size],
-                    mybir.AluOpType.mult,
-                )
-                sums = banks.tile([1, BANK_COLUMNS], F32, name="sums")
-                nc.tensor.matmul(
-                    sums[:, 0:size], ones[:], halves[:, 2 * begin + 1 : 2 * end : 2], start=True, stop=True
-                )
-                nc.scalar.activation(
-                    scores[:, begin:end], sums[:, 0:size], mybir.ActivationFunctionType.Sigmoid
-                )
-                node += size
+        begin = 0
+        for size in PIECES:
+            end = begin + size
+            column = (begin - FIRST) % NODES
+            nc.vector.tensor_tensor(
+                products[:, begin:end],
+                window[:].indirect(offsets[:, begin // OFFSETS_PER_COLUMN : end // OFFSETS_PER_COLUMN]),
+                own[:, column : column + size],
+                mybir.AluOpType.mult,
+            )
+            sums = banks.tile([1, BANK_COLUMNS], F32, name="sums")
+            nc.tensor.matmul(
+                sums[:, 0:size], ones[:], halves[:, 2 * begin + 1 : 2 * end : 2], start=True, stop=True
+            )
+            nc.scalar.activation(
+                scores[:, begin:end], sums[:, 0:size], mybir.ActivationFunctionType.Sigmoid
+            )
+            begin = end
 
         nc.scalar.dma_start(out, scores[:])

@@ -58,4 +58,4 @@ def tile_crossentropy_kernel(tc, x, offs, out):
             )
             begin = end
 
-        nc.scalar.dma_start(out, scores[:])
+        nc.sync.dma_start(out, scores[:])

@@ -13,7 +13,8 @@ FIRST = NODES // 4
 LAST_CUT = [NODES // 2, NODES // 4]
 PIECES = [FIRST] + (PARTNERS - 1) * [NODES] + LAST_CUT
 BANK_COLUMNS = 512
-BANKS_IN_TURN = 4
+SUM_COLUMNS = NODES // 2
+BANKS_IN_TURN = 8
 
 FLOPS = 2 * FEATURES * LIST
 
@@ -49,13 +50,15 @@ def tile_crossentropy_kernel(tc, x, offs, out):
                 own[:, column : column + size],
                 mybir.AluOpType.mult,
             )
-            sums = banks.tile([1, BANK_COLUMNS], F32, name="sums")
-            nc.tensor.matmul(
-                sums[:, 0:size], ones[:], halves[:, 2 * begin + 1 : 2 * end : 2], start=True, stop=True
-            )
-            nc.scalar.activation(
-                scores[:, begin:end], sums[:, 0:size], mybir.ActivationFunctionType.Sigmoid
-            )
+            for low in range(begin, end, SUM_COLUMNS):
+                high = min(low + SUM_COLUMNS, end)
+                sums = banks.tile([1, BANK_COLUMNS], F32, name="sums")
+                nc.tensor.matmul(
+                    sums[:, 0 : high - low], ones[:], halves[:, 2 * low + 1 : 2 * high : 2], start=True, stop=True
+                )
+                nc.scalar.activation(
+                    scores[:, low:high], sums[:, 0 : high - low], mybir.ActivationFunctionType.Sigmoid
+                )
             begin = end
 
         nc.sync.dma_start(out, scores[:])

@@ -16,6 +16,8 @@ BANK_COLUMNS = 512
 SUM_COLUMNS = NODES // 2
 BANKS_IN_TURN = 8
 
+EARLY = LIST - LIST // 4
+
 FLOPS = 2 * FEATURES * LIST
 
 
@@ -61,4 +63,5 @@ def tile_crossentropy_kernel(tc, x, offs, out):
                 )
             begin = end
 
-        nc.sync.dma_start(out, scores[:])
+        for part in (slice(0, EARLY), slice(EARLY, LIST)):
+            nc.sync.dma_start(out[:, part], scores[:, part])

@@ -13,10 +13,10 @@ FIRST = NODES // 4
 LAST_CUT = [NODES // 2, NODES // 4]
 PIECES = [FIRST] + (PARTNERS - 1) * [NODES] + LAST_CUT
 BANK_COLUMNS = 512
-SUM_COLUMNS = NODES // 2
+SUM_COLUMNS = NODES // 4
 BANKS_IN_TURN = 8
 
-EARLY = LIST - LIST // 4
+EARLY = LIST - LIST // 8
 
 FLOPS = 2 * FEATURES * LIST
 
@@ -63,5 +63,5 @@ def tile_crossentropy_kernel(tc, x, offs, out):
                 )
             begin = end
 
-        for part in (slice(0, EARLY), slice(EARLY, LIST)):
+        for part in (slice(0, LIST // 2), slice(LIST // 2, EARLY), slice(EARLY, LIST)):
             nc.sync.dma_start(out[:, part], scores[:, part])

import concourse.mybir as mybir

F32 = mybir.dt.float32
BF16 = mybir.dt.bfloat16
U16 = mybir.dt.uint16

FEATURES = 128
NODES = 256
PARTNERS = 8
LIST = NODES * PARTNERS
OFFSETS_PER_COLUMN = 16
FIRST = NODES // 4
LAST_CUT = [NODES // 2, NODES // 4]
PIECES = [FIRST] + (PARTNERS - 1) * [NODES] + LAST_CUT
BANK_COLUMNS = 512
SUM_COLUMNS = NODES // 4
BANKS_IN_TURN = 8

EARLY = LIST - LIST // 8

FLOPS = 2 * FEATURES * LIST


def tile_crossentropy_kernel(tc, x, offs, out):
    nc = tc.nc
    with (
        tc.tile_pool(name="held", bufs=1) as held,
        tc.psum_pool(name="banks", bufs=BANKS_IN_TURN) as banks,
    ):
        offsets = held.tile([FEATURES, LIST // OFFSETS_PER_COLUMN], U16, name="offsets")
        nc.sync.dma_start(offsets[:], offs)

        window = held.tile([FEATURES, NODES], F32, name="window")
        nc.scalar.dma_start(window[:], x)
        own = held.tile([FEATURES, NODES], F32, name="own")
        nc.sync.dma_start(own[:, NODES - FIRST : NODES], x[:, 0:FIRST])
        nc.scalar.dma_start(own[:, 0 : NODES - FIRST], x[:, FIRST:NODES])

        ones = held.tile([FEATURES, 1], BF16, name="ones")
        nc.gpsimd.memset(ones[:], 1.0)

        products = held.tile([FEATURES, LIST], F32, name="products")
        halves = products[:].bitcast(BF16)
        scores = held.tile([1, LIST], F32, name="scores")
        begin = 0
        for size in PIECES:
            end = begin + size
            column = (begin - FIRST) % NODES
            nc.vector.tensor_tensor(
                products[:, begin:end],
                window[:].indirect(offsets[:, begin // OFFSETS_PER_COLUMN : end // OFFSETS_PER_COLUMN]),
                own[:, column : column + size],
                mybir.AluOpType.mult,
            )
            for low in range(begin, end, SUM_COLUMNS):
                high = min(low + SUM_COLUMNS, end)
                sums = banks.tile([1, BANK_COLUMNS], F32, name="sums")
                nc.tensor.matmul(
                    sums[:, 0 : high - low], ones[:], halves[:, 2 * low + 1 : 2 * high : 2], start=True, stop=True
                )
                nc.scalar.activation(
                    scores[:, low:high], sums[:, 0 : high - low], mybir.ActivationFunctionType.Sigmoid
                )
            begin = end

        for part in (slice(0, LIST // 2), slice(LIST // 2, EARLY), slice(EARLY, LIST)):
            nc.sync.dma_start(out[:, part], scores[:, part])
